import numpy as np
import ml_dtypes


def mxq(x, axis, fmt="e4m3"):
    dtype, down = {"e4m3": (ml_dtypes.float8_e4m3fn, 7), "e5m2": (ml_dtypes.float8_e5m2, 14)}[fmt]
    v = np.moveaxis(np.asarray(x, np.float32).astype(ml_dtypes.bfloat16).astype(np.float64), axis, -1)
    blocks = v.reshape(v.shape[:-1] + (-1, 32))
    amax = np.abs(blocks).max(-1, keepdims=True)
    byte = np.maximum(np.where(amax > 0, np.frexp(amax)[1] - 1 + 127, 0) - down, 1)
    scale = np.exp2(byte - 127.0)
    codes = (blocks / scale).astype(np.float32).astype(dtype).astype(np.float64)
    return np.moveaxis((codes * scale).reshape(v.shape), -1, axis)


WIDE = False


def mx_kscale(k):
    if not WIDE:
        return np.ones(k)
    levels = np.array([10, -10, 5, -5, 0])
    a = np.random.permutation(np.resize(levels, k // 512 * 4)).reshape(k // 512, 4)
    idx = np.arange(k)
    return np.exp2(a[idx // 512, idx % 128 // 32])


BF16 = ml_dtypes.bfloat16


def bf(x):
    return np.asarray(x, np.float32).astype(BF16)


def f64(x):
    return np.asarray(x).astype(np.float64)


B, S, C, H, D = 8, 1024, 512, 2, 128
E = H * D


def rope_tables():
    inv_freq = 1.0 / (10000.0 ** (np.arange(0, D, 2) / D))
    emb = np.repeat(np.outer(np.arange(S), inv_freq), 2, axis=1)
    return np.cos(emb), np.sin(emb)


def rope(t, cos, sin):
    tr = t[..., 0::2]
    ti = t[..., 1::2]
    t_rot = np.stack([-ti, tr], axis=-1).reshape(t.shape)
    return t * cos + t_rot * sin


def setup_inputs():
    s = mx_kscale(C)
    cos, sin = rope_tables()
    return {"x": bf(np.random.standard_normal((B, S, C)) * s),
            "cos": bf(cos), "sin": bf(sin),
            "Wq": bf(np.random.standard_normal((E, C)) / np.sqrt(C) / s[None, :]),
            "bq": bf(np.random.standard_normal(E) * 0.1)}


def reference(x, cos, sin, Wq, bq):
    y = (mxq(f64(x), 2, "e4m3") @ mxq(f64(Wq), 1, "e4m3").T) + f64(bq)
    q = y.reshape(B, S, H, D).transpose(0, 2, 1, 3)
    return np.maximum(rope(q, f64(cos), f64(sin)), 0.0)

@@ -1,0 +1,186 @@
+from contextlib import ExitStack
+
+import concourse.mybir as mybir
+from concourse.masks import make_identity
+
+F32 = mybir.dt.float32
+BF16 = mybir.dt.bfloat16
+U32 = mybir.dt.uint32
+U8 = mybir.dt.uint8
+FP8X4 = mybir.dt.float8_e4m3fn_x4
+ALU = mybir.AluOpType
+ACT = mybir.ActivationFunctionType
+
+B, S, C, H, D = 8, 1024, 512, 2, 128
+P = 128
+PACK = 4
+WORDS = C // 2
+ROWS = S // P
+GROUP_ROWS = 4
+GROUP_TOKENS = GROUP_ROWS * P
+GROUPS = B * ROWS // GROUP_ROWS
+
+FLOPS = 2 * B * S * C * H * D
+
+
+def tile_lineartransformerblock_pa_t_kernel(tc, x, cos, sin, Wq, bq, out):
+    nc = tc.nc
+    with ExitStack() as ctx:
+        const = ctx.enter_context(tc.tile_pool(name="const", bufs=1))
+        tokens = ctx.enter_context(tc.tile_pool(name="tokens", bufs=GROUPS))
+        staged = ctx.enter_context(tc.tile_pool(name="staged", bufs=3))
+        products = ctx.enter_context(tc.tile_pool(name="products", bufs=3))
+        results = ctx.enter_context(tc.tile_pool(name="results", bufs=4))
+        psum_words = ctx.enter_context(tc.psum_pool(name="psum_words", bufs=2))
+        psum_proj = ctx.enter_context(tc.psum_pool(name="psum_proj", bufs=4))
+        psum_rope = ctx.enter_context(tc.psum_pool(name="psum_rope", bufs=2))
+        ctx.enter_context(tc.manual_schedule())
+
+        ident_f32 = const.tile([P, P], F32)
+        make_identity(nc, ident_f32[:])
+        ident_bf16 = const.tile([P, P], BF16)
+        make_identity(nc, ident_bf16[:])
+        swap_f32 = const.tile([P, P], F32)
+        ident_pairs = ident_f32[:].rearrange("k (i two) -> k i two", two=2)
+        swap_pairs = swap_f32[:].rearrange("k (i two) -> k i two", two=2)
+        nc.vector.tensor_copy(out=swap_pairs[:, :, 0], in_=ident_pairs[:, :, 1])
+        nc.vector.tensor_copy(out=swap_pairs[:, :, 1], in_=ident_pairs[:, :, 0])
+        bias_rows = const.tile([P, P], BF16)
+        nc.vector.memset(bias_rows[:], 0.0)
+
+        w_sb = const.tile([P, H, C], BF16)
+        nc.sync.dma_start(out=w_sb[:], in_=Wq.rearrange("(h d) k -> d h k", h=H))
+        nc.sync.dma_start(out=bias_rows[0:H, :], in_=bq.rearrange("(h d) -> h d", h=H))
+
+        x_tiles = {}
+
+        def load_tokens(g):
+            rows = slice((g % 2) * GROUP_ROWS, (g % 2 + 1) * GROUP_ROWS)
+            x_sb = tokens.tile([P, GROUP_ROWS, C], BF16)
+            nc.sync.dma_start(out=x_sb[:], in_=x[g // 2].rearrange("(p j) k -> p j k", j=ROWS)[:, rows, :])
+            x_tiles[g] = x_sb
+
+        load_tokens(0)
+        sin_sb = const.tile([P, ROWS, D], BF16)
+        nc.sync.dma_start(out=sin_sb[:], in_=sin.rearrange("(p j) d -> p j d", j=ROWS))
+        cos_sb = const.tile([P, ROWS, D], BF16)
+        nc.sync.dma_start(out=cos_sb[:], in_=cos.rearrange("(p j) d -> p j d", j=ROWS))
+        for g in range(1, GROUPS):
+            load_tokens(g)
+
+        def words_to_partitions(row_blocks, grouped_words):
+            words_ps = psum_words.tile([P, 2, 2 * P], F32, tag="words")
+            for r, block in enumerate(row_blocks):
+                for u in range(2):
+                    nc.tensor.transpose(words_ps[:, u, r * P : (r + 1) * P], block[:, u * P : (u + 1) * P], ident_f32[:])
+            nc.scalar.copy(out=grouped_words, in_=words_ps[:].rearrange("p u c -> p c u"))
+
+        w_grouped = const.tile([P, H * D * PACK], BF16, align_bytes=64)
+        words_to_partitions(
+            [w_sb[:, h, :].bitcast(F32) for h in range(H)],
+            w_grouped[:].bitcast(F32).rearrange("p (c u) -> p c u", u=2),
+        )
+        w_codes = const.tile([P, H * D], U32, align_bytes=64)
+        w_scales = const.tile([P, H * D], U8, align_bytes=64)
+        nc.vector.quantize_mx(out=w_codes[:].bitcast(FP8X4), scales=w_scales[:], in_=w_grouped[:])
+
+        bias_ps = psum_rope.tile([P, P], BF16, tag="rope")
+        nc.tensor.transpose(bias_ps[:], bias_rows[:], ident_bf16[:])
+        bias = const.tile([P, H], F32)
+        nc.vector.tensor_copy(out=bias[:], in_=bias_ps[:, 0:H])
+
+        grouped_tiles = {}
+        code_tiles = {}
+        proj_tiles = {}
+        product_tiles = {}
+
+        def turn_tokens(g):
+            grouped = staged.tile([P, GROUP_TOKENS * PACK], BF16, align_bytes=64)
+            grouped_words = grouped[:].bitcast(F32).rearrange("p (c u) -> p c u", u=2)
+            for half in range(2):
+                words_to_partitions(
+                    [x_tiles[g][:, 2 * half + r, :].bitcast(F32) for r in range(2)],
+                    grouped_words[:, half * 2 * P : (half + 1) * 2 * P, :],
+                )
+            grouped_tiles[g] = grouped
+
+        def quantise(g):
+            codes = staged.tile([P, GROUP_TOKENS], U32, align_bytes=64)
+            scales = staged.tile([P, GROUP_TOKENS], U8, align_bytes=64)
+            nc.vector.quantize_mx(out=codes[:].bitcast(FP8X4), scales=scales[:], in_=grouped_tiles[g][:])
+            code_tiles[g] = (codes, scales)
+
+        def project(g):
+            codes, scales = code_tiles[g]
+            for h in range(H):
+                head = slice(h * D, (h + 1) * D)
+                y_ps = psum_proj.tile([P, GROUP_TOKENS], F32, tag="proj")
+                nc.tensor.matmul_mx(
+                    out=y_ps[:],
+                    lhsT=w_codes[:, head].bitcast(FP8X4),
+                    lhsT_scale=w_scales[:, head],
+                    rhs=codes[:].bitcast(FP8X4),
+                    rhs_scale=scales[:],
+                    start=True,
+                    stop=True,
+                )
+                proj_tiles[(g, h)] = y_ps
+
+        def rope_products(g, h):
+            cols = slice((g % 2) * GROUP_TOKENS, (g % 2 + 1) * GROUP_TOKENS)
+            y_ps = proj_tiles[(g, h)]
+            own = products.tile([P, GROUP_TOKENS], F32)
+            nc.vector.scalar_tensor_tensor(
+                out=own[:], in0=y_ps[:], scalar=bias[:, h : h + 1], in1=cos_t[:, cols], op0=ALU.add, op1=ALU.mult
+            )
+            lent = products.tile([P, GROUP_TOKENS], F32)
+            nc.vector.scalar_tensor_tensor(
+                out=lent[:], in0=y_ps[:], scalar=bias[:, h : h + 1], in1=sin_lent_t[:, cols], op0=ALU.add, op1=ALU.mult
+            )
+            product_tiles[(g, h)] = (own, lent)
+
+        def finish(g, h):
+            own, lent = product_tiles[(g, h)]
+            rope_ps = psum_rope.tile([P, GROUP_ROWS, D], F32, tag="rope")
+            for j in range(GROUP_ROWS):
+                block = slice(j * P, (j + 1) * P)
+                nc.tensor.matmul(rope_ps[:, j, :], lhsT=own[:, block], rhs=ident_f32[:], is_transpose=True, start=True, stop=False)
+                nc.tensor.matmul(rope_ps[:, j, :], lhsT=lent[:, block], rhs=swap_f32[:], is_transpose=True, start=False, stop=True)
+            out_sb = results.tile([P, GROUP_ROWS, D], F32)
+            nc.scalar.activation(out=out_sb[:], in_=rope_ps[:], func=ACT.Relu)
+            rows = slice((g % 2) * GROUP_ROWS, (g % 2 + 1) * GROUP_ROWS)
+            nc.sync.dma_start(out=out[g // 2, h].rearrange("(p j) d -> p j d", j=ROWS)[:, rows, :], in_=out_sb[:])
+
+        def table_to_channels(table_sb, table_t):
+            table_ps = psum_proj.tile([P, ROWS, P], BF16, tag="proj")
+            for j in range(ROWS):
+                nc.tensor.transpose(table_ps[:, j, :], table_sb[:, j, :], ident_bf16[:])
+            nc.scalar.copy(out=table_t[:], in_=table_ps[:].rearrange("d j p -> d (j p)"))
+
+        turn_tokens(0)
+        cos_t = const.tile([P, S], BF16)
+        table_to_channels(cos_sb, cos_t)
+        turn_tokens(1)
+        sin_lent = const.tile([P, ROWS, D], BF16)
+        sin_pairs = sin_sb[:].rearrange("p j (i two) -> p j i two", two=2)
+        lent_pairs = sin_lent[:].rearrange("p j (i two) -> p j i two", two=2)
+        nc.gpsimd.tensor_scalar(out=lent_pairs[:, :, :, 0], in0=sin_pairs[:, :, :, 1], scalar1=1.0, scalar2=0.0, op0=ALU.mult, op1=ALU.add)
+        nc.gpsimd.tensor_scalar(out=lent_pairs[:, :, :, 1], in0=sin_pairs[:, :, :, 0], scalar1=-1.0, scalar2=0.0, op0=ALU.mult, op1=ALU.add)
+        sin_lent_t = const.tile([P, S], BF16)
+        table_to_channels(sin_lent, sin_lent_t)
+        quantise(0)
+        project(0)
+
+        for g in range(GROUPS):
+            rope_products(g, 0)
+            if g >= 1:
+                finish(g - 1, 1)
+            if g + 2 < GROUPS:
+                turn_tokens(g + 2)
+            if g + 1 < GROUPS:
+                quantise(g + 1)
+            finish(g, 0)
+            if g + 1 < GROUPS:
+                project(g + 1)
+            rope_products(g, 1)
+        finish(GROUPS - 1, 1)

@@ -161,6 +161,8 @@ def tile_lineartransformerblock_pa_t_kernel(tc, x, cos, sin, Wq, bq, out):
         cos_t = const.tile([P, S], BF16)
         table_to_channels(cos_sb, cos_t)
         turn_tokens(1)
+        quantise(0)
+        project(0)
         sin_lent = const.tile([P, ROWS, D], BF16)
         sin_pairs = sin_sb[:].rearrange("p j (i two) -> p j i two", two=2)
         lent_pairs = sin_lent[:].rearrange("p j (i two) -> p j i two", two=2)
@@ -168,19 +170,20 @@ def tile_lineartransformerblock_pa_t_kernel(tc, x, cos, sin, Wq, bq, out):
         nc.gpsimd.tensor_scalar(out=lent_pairs[:, :, :, 1], in0=sin_pairs[:, :, :, 0], scalar1=-1.0, scalar2=0.0, op0=ALU.mult, op1=ALU.add)
         sin_lent_t = const.tile([P, S], BF16)
         table_to_channels(sin_lent, sin_lent_t)
-        quantise(0)
-        project(0)
+        turn_tokens(2)
+        quantise(1)
+        project(1)
 
         for g in range(GROUPS):
             rope_products(g, 0)
             if g >= 1:
                 finish(g - 1, 1)
+            if g + 3 < GROUPS:
+                turn_tokens(g + 3)
             if g + 2 < GROUPS:
-                turn_tokens(g + 2)
-            if g + 1 < GROUPS:
-                quantise(g + 1)
+                quantise(g + 2)
             finish(g, 0)
-            if g + 1 < GROUPS:
-                project(g + 1)
+            if g + 2 < GROUPS:
+                project(g + 2)
             rope_products(g, 1)
         finish(GROUPS - 1, 1)

@@ -12,15 +12,16 @@ ALU = mybir.AluOpType
 ACT = mybir.ActivationFunctionType
 
 B, S, C, H, D = 8, 1024, 512, 2, 128
+E = H * D
 P = 128
 PACK = 4
-WORDS = C // 2
 ROWS = S // P
 GROUP_ROWS = 4
 GROUP_TOKENS = GROUP_ROWS * P
 GROUPS = B * ROWS // GROUP_ROWS
+UNITS = GROUPS * H
 
-FLOPS = 2 * B * S * C * H * D
+FLOPS = 2 * B * S * C * E
 
 
 def tile_lineartransformerblock_pa_t_kernel(tc, x, cos, sin, Wq, bq, out):
@@ -29,80 +30,80 @@ def tile_lineartransformerblock_pa_t_kernel(tc, x, cos, sin, Wq, bq, out):
         const = ctx.enter_context(tc.tile_pool(name="const", bufs=1))
         tokens = ctx.enter_context(tc.tile_pool(name="tokens", bufs=GROUPS))
         staged = ctx.enter_context(tc.tile_pool(name="staged", bufs=3))
-        products = ctx.enter_context(tc.tile_pool(name="products", bufs=3))
+        products = ctx.enter_context(tc.tile_pool(name="products", bufs=4))
         results = ctx.enter_context(tc.tile_pool(name="results", bufs=4))
         psum_words = ctx.enter_context(tc.psum_pool(name="psum_words", bufs=2))
         psum_proj = ctx.enter_context(tc.psum_pool(name="psum_proj", bufs=4))
-        psum_rope = ctx.enter_context(tc.psum_pool(name="psum_rope", bufs=2))
+        psum_back = ctx.enter_context(tc.psum_pool(name="psum_back", bufs=2))
         ctx.enter_context(tc.manual_schedule())
+
+        def pairs(ap):
+            return ap.rearrange("p (i two) -> p i two", two=2)
 
         ident_f32 = const.tile([P, P], F32)
         make_identity(nc, ident_f32[:])
         ident_bf16 = const.tile([P, P], BF16)
         make_identity(nc, ident_bf16[:])
         swap_f32 = const.tile([P, P], F32)
-        ident_pairs = ident_f32[:].rearrange("k (i two) -> k i two", two=2)
-        swap_pairs = swap_f32[:].rearrange("k (i two) -> k i two", two=2)
-        nc.vector.tensor_copy(out=swap_pairs[:, :, 0], in_=ident_pairs[:, :, 1])
-        nc.vector.tensor_copy(out=swap_pairs[:, :, 1], in_=ident_pairs[:, :, 0])
-        bias_rows = const.tile([P, P], BF16)
-        nc.vector.memset(bias_rows[:], 0.0)
+        nc.vector.tensor_copy(out=pairs(swap_f32[:])[:, :, 0], in_=pairs(ident_f32[:])[:, :, 1])
+        nc.vector.tensor_copy(out=pairs(swap_f32[:])[:, :, 1], in_=pairs(ident_f32[:])[:, :, 0])
+        bias_rows = const.tile([P, 2, P], BF16)
+        nc.vector.memset(bias_rows[:, 0, :], 0.0)
 
         w_sb = const.tile([P, H, C], BF16)
         nc.sync.dma_start(out=w_sb[:], in_=Wq.rearrange("(h d) k -> d h k", h=H))
-        nc.sync.dma_start(out=bias_rows[0:H, :], in_=bq.rearrange("(h d) -> h d", h=H))
+        nc.sync.dma_start(out=bias_rows[0:H, 0, :], in_=bq.rearrange("(h d) -> h d", h=H))
+
+        def group_rows(g):
+            return slice((g % 2) * GROUP_ROWS, (g % 2 + 1) * GROUP_ROWS)
 
         x_tiles = {}
 
         def load_tokens(g):
-            rows = slice((g % 2) * GROUP_ROWS, (g % 2 + 1) * GROUP_ROWS)
             x_sb = tokens.tile([P, GROUP_ROWS, C], BF16)
-            nc.sync.dma_start(out=x_sb[:], in_=x[g // 2].rearrange("(p j) k -> p j k", j=ROWS)[:, rows, :])
+            nc.sync.dma_start(out=x_sb[:], in_=x[g // 2].rearrange("(p j) k -> p j k", j=ROWS)[:, group_rows(g), :])
             x_tiles[g] = x_sb
 
         load_tokens(0)
-        sin_sb = const.tile([P, ROWS, D], BF16)
-        nc.sync.dma_start(out=sin_sb[:], in_=sin.rearrange("(p j) d -> p j d", j=ROWS))
         cos_sb = const.tile([P, ROWS, D], BF16)
         nc.sync.dma_start(out=cos_sb[:], in_=cos.rearrange("(p j) d -> p j d", j=ROWS))
+        sin_sb = const.tile([P, ROWS, D], BF16)
+        nc.sync.dma_start(out=sin_sb[:], in_=sin.rearrange("(p j) d -> p j d", j=ROWS))
         for g in range(1, GROUPS):
             load_tokens(g)
 
-        def words_to_partitions(row_blocks, grouped_words):
+        def words_to_partitions(row_blocks, moving, grouped_words):
             words_ps = psum_words.tile([P, 2, 2 * P], F32, tag="words")
             for r, block in enumerate(row_blocks):
                 for u in range(2):
-                    nc.tensor.transpose(words_ps[:, u, r * P : (r + 1) * P], block[:, u * P : (u + 1) * P], ident_f32[:])
+                    nc.tensor.transpose(words_ps[:, u, r * P : (r + 1) * P], block[:, u * P : (u + 1) * P], moving[:])
             nc.scalar.copy(out=grouped_words, in_=words_ps[:].rearrange("p u c -> p c u"))
 
-        w_grouped = const.tile([P, H * D * PACK], BF16, align_bytes=64)
-        words_to_partitions(
-            [w_sb[:, h, :].bitcast(F32) for h in range(H)],
-            w_grouped[:].bitcast(F32).rearrange("p (c u) -> p c u", u=2),
-        )
-        w_codes = const.tile([P, H * D], U32, align_bytes=64)
-        w_scales = const.tile([P, H * D], U8, align_bytes=64)
+        w_grouped = const.tile([P, 2 * E * PACK], BF16, align_bytes=64)
+        w_grouped_words = w_grouped[:].bitcast(F32).rearrange("p (c u) -> p c u", u=2)
+        w_blocks = [w_sb[:, h, :].bitcast(F32) for h in range(H)]
+        words_to_partitions(w_blocks, ident_f32, w_grouped_words[:, 0:E, :])
+        words_to_partitions(w_blocks, swap_f32, w_grouped_words[:, E : 2 * E, :])
+        w_codes = const.tile([P, 2 * E], U32, align_bytes=64)
+        w_scales = const.tile([P, 2 * E], U8, align_bytes=64)
         nc.vector.quantize_mx(out=w_codes[:].bitcast(FP8X4), scales=w_scales[:], in_=w_grouped[:])
-
-        bias_ps = psum_rope.tile([P, P], BF16, tag="rope")
-        nc.tensor.transpose(bias_ps[:], bias_rows[:], ident_bf16[:])
-        bias = const.tile([P, H], F32)
-        nc.vector.tensor_copy(out=bias[:], in_=bias_ps[:, 0:H])
 
         grouped_tiles = {}
         code_tiles = {}
         proj_tiles = {}
         product_tiles = {}
+        rotated_tiles = {}
 
-        def turn_tokens(g):
-            grouped = staged.tile([P, GROUP_TOKENS * PACK], BF16, align_bytes=64)
-            grouped_words = grouped[:].bitcast(F32).rearrange("p (c u) -> p c u", u=2)
-            for half in range(2):
-                words_to_partitions(
-                    [x_tiles[g][:, 2 * half + r, :].bitcast(F32) for r in range(2)],
-                    grouped_words[:, half * 2 * P : (half + 1) * 2 * P, :],
-                )
-            grouped_tiles[g] = grouped
+        def turn_tokens(g, half):
+            if half == 0:
+                grouped = staged.tile([P, GROUP_TOKENS * PACK], BF16, align_bytes=64)
+                grouped_tiles[g] = grouped
+            grouped_words = grouped_tiles[g][:].bitcast(F32).rearrange("p (c u) -> p c u", u=2)
+            words_to_partitions(
+                [x_tiles[g][:, 2 * half + r, :].bitcast(F32) for r in range(2)],
+                ident_f32,
+                grouped_words[:, half * 2 * P : (half + 1) * 2 * P, :],
+            )
 
         def quantise(g):
             codes = staged.tile([P, GROUP_TOKENS], U32, align_bytes=64)
@@ -110,46 +111,62 @@ def tile_lineartransformerblock_pa_t_kernel(tc, x, cos, sin, Wq, bq, out):
             nc.vector.quantize_mx(out=codes[:].bitcast(FP8X4), scales=scales[:], in_=grouped_tiles[g][:])
             code_tiles[g] = (codes, scales)
 
-        def project(g):
+        def project(g, h):
             codes, scales = code_tiles[g]
-            for h in range(H):
-                head = slice(h * D, (h + 1) * D)
+            banks = []
+            for v in range(2):
+                rows = slice(v * E + h * D, v * E + (h + 1) * D)
                 y_ps = psum_proj.tile([P, GROUP_TOKENS], F32, tag="proj")
                 nc.tensor.matmul_mx(
                     out=y_ps[:],
-                    lhsT=w_codes[:, head].bitcast(FP8X4),
-                    lhsT_scale=w_scales[:, head],
+                    lhsT=w_codes[:, rows].bitcast(FP8X4),
+                    lhsT_scale=w_scales[:, rows],
                     rhs=codes[:].bitcast(FP8X4),
                     rhs_scale=scales[:],
                     start=True,
                     stop=True,
                 )
-                proj_tiles[(g, h)] = y_ps
+                banks.append(y_ps)
+            proj_tiles[(g, h)] = banks
 
         def rope_products(g, h):
             cols = slice((g % 2) * GROUP_TOKENS, (g % 2 + 1) * GROUP_TOKENS)
-            y_ps = proj_tiles[(g, h)]
+            y_ps, y_partner_ps = proj_tiles[(g, h)]
             own = products.tile([P, GROUP_TOKENS], F32)
             nc.vector.scalar_tensor_tensor(
-                out=own[:], in0=y_ps[:], scalar=bias[:, h : h + 1], in1=cos_t[:, cols], op0=ALU.add, op1=ALU.mult
+                out=own[:], in0=y_ps[:], scalar=bias[:, 0, h : h + 1], in1=cos_t[:, cols], op0=ALU.add, op1=ALU.mult
             )
             lent = products.tile([P, GROUP_TOKENS], F32)
             nc.vector.scalar_tensor_tensor(
-                out=lent[:], in0=y_ps[:], scalar=bias[:, h : h + 1], in1=sin_lent_t[:, cols], op0=ALU.add, op1=ALU.mult
+                out=lent[:], in0=y_partner_ps[:], scalar=bias[:, 1, h : h + 1], in1=sin_t[:, cols], op0=ALU.add, op1=ALU.mult
             )
             product_tiles[(g, h)] = (own, lent)
 
-        def finish(g, h):
+        def rotate(g, h):
             own, lent = product_tiles[(g, h)]
-            rope_ps = psum_rope.tile([P, GROUP_ROWS, D], F32, tag="rope")
+            rotated = products.tile([P, GROUP_TOKENS], F32)
+            nc.gpsimd.tensor_tensor(out=rotated[:], in0=own[:], in1=lent[:], op=ALU.add)
+            rotated_tiles[(g, h)] = rotated
+
+        def finish(g, h):
+            rotated = rotated_tiles[(g, h)]
+            back_ps = psum_back.tile([P, GROUP_ROWS, D], F32, tag="back")
             for j in range(GROUP_ROWS):
-                block = slice(j * P, (j + 1) * P)
-                nc.tensor.matmul(rope_ps[:, j, :], lhsT=own[:, block], rhs=ident_f32[:], is_transpose=True, start=True, stop=False)
-                nc.tensor.matmul(rope_ps[:, j, :], lhsT=lent[:, block], rhs=swap_f32[:], is_transpose=True, start=False, stop=True)
+                nc.tensor.transpose(back_ps[:, j, :], rotated[:, j * P : (j + 1) * P], ident_f32[:])
             out_sb = results.tile([P, GROUP_ROWS, D], F32)
-            nc.scalar.activation(out=out_sb[:], in_=rope_ps[:], func=ACT.Relu)
-            rows = slice((g % 2) * GROUP_ROWS, (g % 2 + 1) * GROUP_ROWS)
-            nc.sync.dma_start(out=out[g // 2, h].rearrange("(p j) d -> p j d", j=ROWS)[:, rows, :], in_=out_sb[:])
+            nc.scalar.activation(out=out_sb[:], in_=back_ps[:], func=ACT.Relu)
+            nc.sync.dma_start(out=out[g // 2, h].rearrange("(p j) d -> p j d", j=ROWS)[:, group_rows(g), :], in_=out_sb[:])
+
+        turn_tokens(0, 0)
+        turn_tokens(0, 1)
+
+        nc.vector.tensor_copy(out=pairs(bias_rows[:, 1, :])[:, :, 0], in_=pairs(bias_rows[:, 0, :])[:, :, 1])
+        nc.vector.tensor_copy(out=pairs(bias_rows[:, 1, :])[:, :, 1], in_=pairs(bias_rows[:, 0, :])[:, :, 0])
+        bias_ps = psum_back.tile([P, 2, P], BF16, tag="back")
+        for v in range(2):
+            nc.tensor.transpose(bias_ps[:, v, :], bias_rows[:, v, :], ident_bf16[:])
+        bias = const.tile([P, 2, H], F32)
+        nc.vector.tensor_copy(out=bias[:], in_=bias_ps[:, :, 0:H])
 
         def table_to_channels(table_sb, table_t):
             table_ps = psum_proj.tile([P, ROWS, P], BF16, tag="proj")
@@ -157,33 +174,29 @@ def tile_lineartransformerblock_pa_t_kernel(tc, x, cos, sin, Wq, bq, out):
                 nc.tensor.transpose(table_ps[:, j, :], table_sb[:, j, :], ident_bf16[:])
             nc.scalar.copy(out=table_t[:], in_=table_ps[:].rearrange("d j p -> d (j p)"))
 
-        turn_tokens(0)
         cos_t = const.tile([P, S], BF16)
         table_to_channels(cos_sb, cos_t)
-        turn_tokens(1)
-        quantise(0)
-        project(0)
-        sin_lent = const.tile([P, ROWS, D], BF16)
-        sin_pairs = sin_sb[:].rearrange("p j (i two) -> p j i two", two=2)
-        lent_pairs = sin_lent[:].rearrange("p j (i two) -> p j i two", two=2)
-        nc.gpsimd.tensor_scalar(out=lent_pairs[:, :, :, 0], in0=sin_pairs[:, :, :, 1], scalar1=1.0, scalar2=0.0, op0=ALU.mult, op1=ALU.add)
-        nc.gpsimd.tensor_scalar(out=lent_pairs[:, :, :, 1], in0=sin_pairs[:, :, :, 0], scalar1=-1.0, scalar2=0.0, op0=ALU.mult, op1=ALU.add)
-        sin_lent_t = const.tile([P, S], BF16)
-        table_to_channels(sin_lent, sin_lent_t)
-        turn_tokens(2)
-        quantise(1)
-        project(1)
+        sin_even = sin_sb[:].rearrange("p j (i two) -> p j i two", two=2)[:, :, :, 0]
+        nc.gpsimd.tensor_scalar(out=sin_even, in0=sin_even, scalar1=-1.0, scalar2=0.0, op0=ALU.mult, op1=ALU.add)
+        sin_t = const.tile([P, S], BF16)
+        table_to_channels(sin_sb, sin_t)
 
-        for g in range(GROUPS):
-            rope_products(g, 0)
-            if g >= 1:
-                finish(g - 1, 1)
-            if g + 3 < GROUPS:
-                turn_tokens(g + 3)
+        quantise(0)
+        project(0, 0)
+        turn_tokens(1, 0)
+        turn_tokens(1, 1)
+
+        for unit in range(UNITS):
+            g, h = divmod(unit, H)
+            rope_products(g, h)
+            rotate(g, h)
+            if unit + 1 < UNITS:
+                project(*divmod(unit + 1, H))
             if g + 2 < GROUPS:
-                quantise(g + 2)
-            finish(g, 0)
-            if g + 2 < GROUPS:
-                project(g + 2)
-            rope_products(g, 1)
-        finish(GROUPS - 1, 1)
+                turn_tokens(g + 2, h)
+            if unit >= 2:
+                finish(*divmod(unit - 2, H))
+            if h == 0 and g + 1 < GROUPS:
+                quantise(g + 1)
+        finish(*divmod(UNITS - 2, H))
+        finish(*divmod(UNITS - 1, H))

@@ -12,16 +12,15 @@ ALU = mybir.AluOpType
 ACT = mybir.ActivationFunctionType
 
 B, S, C, H, D = 8, 1024, 512, 2, 128
-E = H * D
 P = 128
 PACK = 4
+WORDS = C // 2
 ROWS = S // P
 GROUP_ROWS = 4
 GROUP_TOKENS = GROUP_ROWS * P
 GROUPS = B * ROWS // GROUP_ROWS
-UNITS = GROUPS * H
 
-FLOPS = 2 * B * S * C * E
+FLOPS = 2 * B * S * C * H * D
 
 
 def tile_lineartransformerblock_pa_t_kernel(tc, x, cos, sin, Wq, bq, out):
@@ -30,80 +29,81 @@ def tile_lineartransformerblock_pa_t_kernel(tc, x, cos, sin, Wq, bq, out):
         const = ctx.enter_context(tc.tile_pool(name="const", bufs=1))
         tokens = ctx.enter_context(tc.tile_pool(name="tokens", bufs=GROUPS))
         staged = ctx.enter_context(tc.tile_pool(name="staged", bufs=3))
-        products = ctx.enter_context(tc.tile_pool(name="products", bufs=4))
+        products = ctx.enter_context(tc.tile_pool(name="products", bufs=3))
         results = ctx.enter_context(tc.tile_pool(name="results", bufs=4))
         psum_words = ctx.enter_context(tc.psum_pool(name="psum_words", bufs=2))
         psum_proj = ctx.enter_context(tc.psum_pool(name="psum_proj", bufs=4))
-        psum_back = ctx.enter_context(tc.psum_pool(name="psum_back", bufs=2))
+        psum_rope = ctx.enter_context(tc.psum_pool(name="psum_rope", bufs=2))
         ctx.enter_context(tc.manual_schedule())
-
-        def pairs(ap):
-            return ap.rearrange("p (i two) -> p i two", two=2)
 
         ident_f32 = const.tile([P, P], F32)
         make_identity(nc, ident_f32[:])
         ident_bf16 = const.tile([P, P], BF16)
         make_identity(nc, ident_bf16[:])
         swap_f32 = const.tile([P, P], F32)
-        nc.vector.tensor_copy(out=pairs(swap_f32[:])[:, :, 0], in_=pairs(ident_f32[:])[:, :, 1])
-        nc.vector.tensor_copy(out=pairs(swap_f32[:])[:, :, 1], in_=pairs(ident_f32[:])[:, :, 0])
-        bias_rows = const.tile([P, 2, P], BF16)
-        nc.vector.memset(bias_rows[:, 0, :], 0.0)
+        ident_pairs = ident_f32[:].rearrange("k (i two) -> k i two", two=2)
+        swap_pairs = swap_f32[:].rearrange("k (i two) -> k i two", two=2)
+        nc.vector.tensor_copy(out=swap_pairs[:, :, 0], in_=ident_pairs[:, :, 1])
+        nc.vector.tensor_copy(out=swap_pairs[:, :, 1], in_=ident_pairs[:, :, 0])
+        bias_rows = const.tile([P, P], BF16)
+        nc.vector.memset(bias_rows[:], 0.0)
 
         w_sb = const.tile([P, H, C], BF16)
         nc.sync.dma_start(out=w_sb[:], in_=Wq.rearrange("(h d) k -> d h k", h=H))
-        nc.sync.dma_start(out=bias_rows[0:H, 0, :], in_=bq.rearrange("(h d) -> h d", h=H))
-
-        def group_rows(g):
-            return slice((g % 2) * GROUP_ROWS, (g % 2 + 1) * GROUP_ROWS)
+        nc.sync.dma_start(out=bias_rows[0:H, :], in_=bq.rearrange("(h d) -> h d", h=H))
 
         x_tiles = {}
 
         def load_tokens(g):
+            rows = slice((g % 2) * GROUP_ROWS, (g % 2 + 1) * GROUP_ROWS)
             x_sb = tokens.tile([P, GROUP_ROWS, C], BF16)
-            nc.sync.dma_start(out=x_sb[:], in_=x[g // 2].rearrange("(p j) k -> p j k", j=ROWS)[:, group_rows(g), :])
+            nc.sync.dma_start(out=x_sb[:], in_=x[g // 2].rearrange("(p j) k -> p j k", j=ROWS)[:, rows, :])
             x_tiles[g] = x_sb
 
         load_tokens(0)
-        cos_sb = const.tile([P, ROWS, D], BF16)
-        nc.sync.dma_start(out=cos_sb[:], in_=cos.rearrange("(p j) d -> p j d", j=ROWS))
         sin_sb = const.tile([P, ROWS, D], BF16)
         nc.sync.dma_start(out=sin_sb[:], in_=sin.rearrange("(p j) d -> p j d", j=ROWS))
+        cos_sb = const.tile([P, ROWS, D], BF16)
+        nc.sync.dma_start(out=cos_sb[:], in_=cos.rearrange("(p j) d -> p j d", j=ROWS))
         for g in range(1, GROUPS):
             load_tokens(g)
 
-        def words_to_partitions(row_blocks, moving, grouped_words):
+        def words_to_partitions(row_blocks, grouped_words):
             words_ps = psum_words.tile([P, 2, 2 * P], F32, tag="words")
             for r, block in enumerate(row_blocks):
                 for u in range(2):
-                    nc.tensor.transpose(words_ps[:, u, r * P : (r + 1) * P], block[:, u * P : (u + 1) * P], moving[:])
+                    nc.tensor.transpose(words_ps[:, u, r * P : (r + 1) * P], block[:, u * P : (u + 1) * P], ident_f32[:])
             nc.scalar.copy(out=grouped_words, in_=words_ps[:].rearrange("p u c -> p c u"))
 
-        w_grouped = const.tile([P, 2 * E * PACK], BF16, align_bytes=64)
-        w_grouped_words = w_grouped[:].bitcast(F32).rearrange("p (c u) -> p c u", u=2)
-        w_blocks = [w_sb[:, h, :].bitcast(F32) for h in range(H)]
-        words_to_partitions(w_blocks, ident_f32, w_grouped_words[:, 0:E, :])
-        words_to_partitions(w_blocks, swap_f32, w_grouped_words[:, E : 2 * E, :])
-        w_codes = const.tile([P, 2 * E], U32, align_bytes=64)
-        w_scales = const.tile([P, 2 * E], U8, align_bytes=64)
+        w_grouped = const.tile([P, H * D * PACK], BF16, align_bytes=64)
+        words_to_partitions(
+            [w_sb[:, h, :].bitcast(F32) for h in range(H)],
+            w_grouped[:].bitcast(F32).rearrange("p (c u) -> p c u", u=2),
+        )
+        w_codes = const.tile([P, H * D], U32, align_bytes=64)
+        w_scales = const.tile([P, H * D], U8, align_bytes=64)
         nc.vector.quantize_mx(out=w_codes[:].bitcast(FP8X4), scales=w_scales[:], in_=w_grouped[:])
+
+        bias_ps = psum_rope.tile([P, P], BF16, tag="rope")
+        nc.tensor.transpose(bias_ps[:], bias_rows[:], ident_bf16[:])
+        bias = const.tile([P, H], F32)
+        nc.vector.tensor_copy(out=bias[:], in_=bias_ps[:, 0:H])
 
         grouped_tiles = {}
         code_tiles = {}
         proj_tiles = {}
-        product_tiles = {}
-        rotated_tiles = {}
+        own_tiles = {}
+        lent_tiles = {}
 
-        def turn_tokens(g, half):
-            if half == 0:
-                grouped = staged.tile([P, GROUP_TOKENS * PACK], BF16, align_bytes=64)
-                grouped_tiles[g] = grouped
-            grouped_words = grouped_tiles[g][:].bitcast(F32).rearrange("p (c u) -> p c u", u=2)
-            words_to_partitions(
-                [x_tiles[g][:, 2 * half + r, :].bitcast(F32) for r in range(2)],
-                ident_f32,
-                grouped_words[:, half * 2 * P : (half + 1) * 2 * P, :],
-            )
+        def turn_tokens(g):
+            grouped = staged.tile([P, GROUP_TOKENS * PACK], BF16, align_bytes=64)
+            grouped_words = grouped[:].bitcast(F32).rearrange("p (c u) -> p c u", u=2)
+            for half in range(2):
+                words_to_partitions(
+                    [x_tiles[g][:, 2 * half + r, :].bitcast(F32) for r in range(2)],
+                    grouped_words[:, half * 2 * P : (half + 1) * 2 * P, :],
+                )
+            grouped_tiles[g] = grouped
 
         def quantise(g):
             codes = staged.tile([P, GROUP_TOKENS], U32, align_bytes=64)
@@ -111,62 +111,68 @@ def tile_lineartransformerblock_pa_t_kernel(tc, x, cos, sin, Wq, bq, out):
             nc.vector.quantize_mx(out=codes[:].bitcast(FP8X4), scales=scales[:], in_=grouped_tiles[g][:])
             code_tiles[g] = (codes, scales)
 
-        def project(g, h):
+        def project(g):
             codes, scales = code_tiles[g]
-            banks = []
-            for v in range(2):
-                rows = slice(v * E + h * D, v * E + (h + 1) * D)
+            for h in range(H):
+                head = slice(h * D, (h + 1) * D)
                 y_ps = psum_proj.tile([P, GROUP_TOKENS], F32, tag="proj")
                 nc.tensor.matmul_mx(
                     out=y_ps[:],
-                    lhsT=w_codes[:, rows].bitcast(FP8X4),
-                    lhsT_scale=w_scales[:, rows],
+                    lhsT=w_codes[:, head].bitcast(FP8X4),
+                    lhsT_scale=w_scales[:, head],
                     rhs=codes[:].bitcast(FP8X4),
                     rhs_scale=scales[:],
                     start=True,
                     stop=True,
                 )
-                banks.append(y_ps)
-            proj_tiles[(g, h)] = banks
+                proj_tiles[(g, h)] = y_ps
 
-        def rope_products(g, h):
-            cols = slice((g % 2) * GROUP_TOKENS, (g % 2 + 1) * GROUP_TOKENS)
-            y_ps, y_partner_ps = proj_tiles[(g, h)]
+        def table_columns(g):
+            return slice((g % 2) * GROUP_TOKENS, (g % 2 + 1) * GROUP_TOKENS)
+
+        def own_product(g, h):
             own = products.tile([P, GROUP_TOKENS], F32)
             nc.vector.scalar_tensor_tensor(
-                out=own[:], in0=y_ps[:], scalar=bias[:, 0, h : h + 1], in1=cos_t[:, cols], op0=ALU.add, op1=ALU.mult
+                out=own[:],
+                in0=proj_tiles[(g, h)][:],
+                scalar=bias[:, h : h + 1],
+                in1=cos_t[:, table_columns(g)],
+                op0=ALU.add,
+                op1=ALU.mult,
             )
+            own_tiles[(g, h)] = own
+
+        def lent_product(g, h):
             lent = products.tile([P, GROUP_TOKENS], F32)
             nc.vector.scalar_tensor_tensor(
-                out=lent[:], in0=y_partner_ps[:], scalar=bias[:, 1, h : h + 1], in1=sin_t[:, cols], op0=ALU.add, op1=ALU.mult
+                out=lent[:],
+                in0=proj_tiles[(g, h)][:],
+                scalar=bias[:, h : h + 1],
+                in1=sin_lent_t[:, table_columns(g)],
+                op0=ALU.add,
+                op1=ALU.mult,
             )
-            product_tiles[(g, h)] = (own, lent)
+            lent_tiles[(g, h)] = lent
 
-        def rotate(g, h):
-            own, lent = product_tiles[(g, h)]
-            rotated = products.tile([P, GROUP_TOKENS], F32)
-            nc.gpsimd.tensor_tensor(out=rotated[:], in0=own[:], in1=lent[:], op=ALU.add)
-            rotated_tiles[(g, h)] = rotated
+        def lent_product_beside_vector(g, h):
+            biased = products.tile([P, GROUP_TOKENS], F32)
+            nc.scalar.activation(out=biased[:], in_=proj_tiles[(g, h)][:], func=ACT.Identity, bias=bias[:, h : h + 1], scale=1.0)
+            lent = products.tile([P, GROUP_TOKENS], F32)
+            nc.gpsimd.tensor_tensor(out=lent[:], in0=biased[:], in1=sin_lent_t[:, table_columns(g)], op=ALU.mult)
+            lent_tiles[(g, h)] = lent
 
         def finish(g, h):
-            rotated = rotated_tiles[(g, h)]
-            back_ps = psum_back.tile([P, GROUP_ROWS, D], F32, tag="back")
+            own = own_tiles[(g, h)]
+            lent = lent_tiles[(g, h)]
+            rope_ps = psum_rope.tile([P, GROUP_ROWS, D], F32, tag="rope")
             for j in range(GROUP_ROWS):
-                nc.tensor.transpose(back_ps[:, j, :], rotated[:, j * P : (j + 1) * P], ident_f32[:])
+                block = slice(j * P, (j + 1) * P)
+                nc.tensor.matmul(rope_ps[:, j, :], lhsT=own[:, block], rhs=ident_f32[:], is_transpose=True, start=True, stop=False)
+                nc.tensor.matmul(rope_ps[:, j, :], lhsT=lent[:, block], rhs=swap_f32[:], is_transpose=True, start=False, stop=True)
             out_sb = results.tile([P, GROUP_ROWS, D], F32)
-            nc.scalar.activation(out=out_sb[:], in_=back_ps[:], func=ACT.Relu)
-            nc.sync.dma_start(out=out[g // 2, h].rearrange("(p j) d -> p j d", j=ROWS)[:, group_rows(g), :], in_=out_sb[:])
-
-        turn_tokens(0, 0)
-        turn_tokens(0, 1)
-
-        nc.vector.tensor_copy(out=pairs(bias_rows[:, 1, :])[:, :, 0], in_=pairs(bias_rows[:, 0, :])[:, :, 1])
-        nc.vector.tensor_copy(out=pairs(bias_rows[:, 1, :])[:, :, 1], in_=pairs(bias_rows[:, 0, :])[:, :, 0])
-        bias_ps = psum_back.tile([P, 2, P], BF16, tag="back")
-        for v in range(2):
-            nc.tensor.transpose(bias_ps[:, v, :], bias_rows[:, v, :], ident_bf16[:])
-        bias = const.tile([P, 2, H], F32)
-        nc.vector.tensor_copy(out=bias[:], in_=bias_ps[:, :, 0:H])
+            nc.scalar.activation(out=out_sb[:], in_=rope_ps[:], func=ACT.Relu)
+            rows = slice((g % 2) * GROUP_ROWS, (g % 2 + 1) * GROUP_ROWS)
+            nc.sync.dma_start(out=out[g // 2, h].rearrange("(p j) d -> p j d", j=ROWS)[:, rows, :], in_=out_sb[:])
 
         def table_to_channels(table_sb, table_t):
             table_ps = psum_proj.tile([P, ROWS, P], BF16, tag="proj")
@@ -174,29 +180,35 @@ def tile_lineartransformerblock_pa_t_kernel(tc, x, cos, sin, Wq, bq, out):
                 nc.tensor.transpose(table_ps[:, j, :], table_sb[:, j, :], ident_bf16[:])
             nc.scalar.copy(out=table_t[:], in_=table_ps[:].rearrange("d j p -> d (j p)"))
 
+        turn_tokens(0)
         cos_t = const.tile([P, S], BF16)
         table_to_channels(cos_sb, cos_t)
-        sin_even = sin_sb[:].rearrange("p j (i two) -> p j i two", two=2)[:, :, :, 0]
-        nc.gpsimd.tensor_scalar(out=sin_even, in0=sin_even, scalar1=-1.0, scalar2=0.0, op0=ALU.mult, op1=ALU.add)
-        sin_t = const.tile([P, S], BF16)
-        table_to_channels(sin_sb, sin_t)
-
+        turn_tokens(1)
         quantise(0)
-        project(0, 0)
-        turn_tokens(1, 0)
-        turn_tokens(1, 1)
+        project(0)
+        sin_lent = const.tile([P, ROWS, D], BF16)
+        sin_pairs = sin_sb[:].rearrange("p j (i two) -> p j i two", two=2)
+        lent_pairs = sin_lent[:].rearrange("p j (i two) -> p j i two", two=2)
+        nc.gpsimd.tensor_scalar(out=lent_pairs[:, :, :, 0], in0=sin_pairs[:, :, :, 1], scalar1=1.0, scalar2=0.0, op0=ALU.mult, op1=ALU.add)
+        nc.gpsimd.tensor_scalar(out=lent_pairs[:, :, :, 1], in0=sin_pairs[:, :, :, 0], scalar1=-1.0, scalar2=0.0, op0=ALU.mult, op1=ALU.add)
+        sin_lent_t = const.tile([P, S], BF16)
+        table_to_channels(sin_lent, sin_lent_t)
+        turn_tokens(2)
+        quantise(1)
+        project(1)
 
-        for unit in range(UNITS):
-            g, h = divmod(unit, H)
-            rope_products(g, h)
-            rotate(g, h)
-            if unit + 1 < UNITS:
-                project(*divmod(unit + 1, H))
+        for g in range(GROUPS):
+            lent_product_beside_vector(g, 1)
+            own_product(g, 0)
+            lent_product(g, 0)
+            if g >= 1:
+                finish(g - 1, 1)
+            if g + 3 < GROUPS:
+                turn_tokens(g + 3)
             if g + 2 < GROUPS:
-                turn_tokens(g + 2, h)
-            if unit >= 2:
-                finish(*divmod(unit - 2, H))
-            if h == 0 and g + 1 < GROUPS:
-                quantise(g + 1)
-        finish(*divmod(UNITS - 2, H))
-        finish(*divmod(UNITS - 1, H))
+                quantise(g + 2)
+            finish(g, 0)
+            if g + 2 < GROUPS:
+                project(g + 2)
+            own_product(g, 1)
+        finish(GROUPS - 1, 1)

from contextlib import ExitStack

import concourse.mybir as mybir
from concourse.masks import make_identity

F32 = mybir.dt.float32
BF16 = mybir.dt.bfloat16
U32 = mybir.dt.uint32
U8 = mybir.dt.uint8
FP8X4 = mybir.dt.float8_e4m3fn_x4
ALU = mybir.AluOpType
ACT = mybir.ActivationFunctionType

B, S, C, H, D = 8, 1024, 512, 2, 128
P = 128
PACK = 4
WORDS = C // 2
ROWS = S // P
GROUP_ROWS = 4
GROUP_TOKENS = GROUP_ROWS * P
GROUPS = B * ROWS // GROUP_ROWS

FLOPS = 2 * B * S * C * H * D


def tile_lineartransformerblock_pa_t_kernel(tc, x, cos, sin, Wq, bq, out):
    nc = tc.nc
    with ExitStack() as ctx:
        const = ctx.enter_context(tc.tile_pool(name="const", bufs=1))
        tokens = ctx.enter_context(tc.tile_pool(name="tokens", bufs=GROUPS))
        staged = ctx.enter_context(tc.tile_pool(name="staged", bufs=3))
        products = ctx.enter_context(tc.tile_pool(name="products", bufs=3))
        results = ctx.enter_context(tc.tile_pool(name="results", bufs=4))
        psum_words = ctx.enter_context(tc.psum_pool(name="psum_words", bufs=2))
        psum_proj = ctx.enter_context(tc.psum_pool(name="psum_proj", bufs=4))
        psum_rope = ctx.enter_context(tc.psum_pool(name="psum_rope", bufs=2))
        ctx.enter_context(tc.manual_schedule())

        ident_f32 = const.tile([P, P], F32)
        make_identity(nc, ident_f32[:])
        ident_bf16 = const.tile([P, P], BF16)
        make_identity(nc, ident_bf16[:])
        swap_f32 = const.tile([P, P], F32)
        ident_pairs = ident_f32[:].rearrange("k (i two) -> k i two", two=2)
        swap_pairs = swap_f32[:].rearrange("k (i two) -> k i two", two=2)
        nc.vector.tensor_copy(out=swap_pairs[:, :, 0], in_=ident_pairs[:, :, 1])
        nc.vector.tensor_copy(out=swap_pairs[:, :, 1], in_=ident_pairs[:, :, 0])
        bias_rows = const.tile([P, P], BF16)
        nc.vector.memset(bias_rows[:], 0.0)

        w_sb = const.tile([P, H, C], BF16)
        nc.sync.dma_start(out=w_sb[:], in_=Wq.rearrange("(h d) k -> d h k", h=H))
        nc.sync.dma_start(out=bias_rows[0:H, :], in_=bq.rearrange("(h d) -> h d", h=H))

        x_tiles = {}

        def load_tokens(g):
            rows = slice((g % 2) * GROUP_ROWS, (g % 2 + 1) * GROUP_ROWS)
            x_sb = tokens.tile([P, GROUP_ROWS, C], BF16)
            nc.sync.dma_start(out=x_sb[:], in_=x[g // 2].rearrange("(p j) k -> p j k", j=ROWS)[:, rows, :])
            x_tiles[g] = x_sb

        load_tokens(0)
        sin_sb = const.tile([P, ROWS, D], BF16)
        nc.sync.dma_start(out=sin_sb[:], in_=sin.rearrange("(p j) d -> p j d", j=ROWS))
        cos_sb = const.tile([P, ROWS, D], BF16)
        nc.sync.dma_start(out=cos_sb[:], in_=cos.rearrange("(p j) d -> p j d", j=ROWS))
        for g in range(1, GROUPS):
            load_tokens(g)

        def words_to_partitions(row_blocks, grouped_words):
            words_ps = psum_words.tile([P, 2, 2 * P], F32, tag="words")
            for r, block in enumerate(row_blocks):
                for u in range(2):
                    nc.tensor.transpose(words_ps[:, u, r * P : (r + 1) * P], block[:, u * P : (u + 1) * P], ident_f32[:])
            nc.scalar.copy(out=grouped_words, in_=words_ps[:].rearrange("p u c -> p c u"))

        w_grouped = const.tile([P, H * D * PACK], BF16, align_bytes=64)
        words_to_partitions(
            [w_sb[:, h, :].bitcast(F32) for h in range(H)],
            w_grouped[:].bitcast(F32).rearrange("p (c u) -> p c u", u=2),
        )
        w_codes = const.tile([P, H * D], U32, align_bytes=64)
        w_scales = const.tile([P, H * D], U8, align_bytes=64)
        nc.vector.quantize_mx(out=w_codes[:].bitcast(FP8X4), scales=w_scales[:], in_=w_grouped[:])

        bias_ps = psum_rope.tile([P, P], BF16, tag="rope")
        nc.tensor.transpose(bias_ps[:], bias_rows[:], ident_bf16[:])
        bias = const.tile([P, H], F32)
        nc.vector.tensor_copy(out=bias[:], in_=bias_ps[:, 0:H])

        grouped_tiles = {}
        code_tiles = {}
        proj_tiles = {}
        own_tiles = {}
        lent_tiles = {}

        def turn_tokens(g):
            grouped = staged.tile([P, GROUP_TOKENS * PACK], BF16, align_bytes=64)
            grouped_words = grouped[:].bitcast(F32).rearrange("p (c u) -> p c u", u=2)
            for half in range(2):
                words_to_partitions(
                    [x_tiles[g][:, 2 * half + r, :].bitcast(F32) for r in range(2)],
                    grouped_words[:, half * 2 * P : (half + 1) * 2 * P, :],
                )
            grouped_tiles[g] = grouped

        def quantise(g):
            codes = staged.tile([P, GROUP_TOKENS], U32, align_bytes=64)
            scales = staged.tile([P, GROUP_TOKENS], U8, align_bytes=64)
            nc.vector.quantize_mx(out=codes[:].bitcast(FP8X4), scales=scales[:], in_=grouped_tiles[g][:])
            code_tiles[g] = (codes, scales)

        def project(g):
            codes, scales = code_tiles[g]
            for h in range(H):
                head = slice(h * D, (h + 1) * D)
                y_ps = psum_proj.tile([P, GROUP_TOKENS], F32, tag="proj")
                nc.tensor.matmul_mx(
                    out=y_ps[:],
                    lhsT=w_codes[:, head].bitcast(FP8X4),
                    lhsT_scale=w_scales[:, head],
                    rhs=codes[:].bitcast(FP8X4),
                    rhs_scale=scales[:],
                    start=True,
                    stop=True,
                )
                proj_tiles[(g, h)] = y_ps

        def table_columns(g):
            return slice((g % 2) * GROUP_TOKENS, (g % 2 + 1) * GROUP_TOKENS)

        def own_product(g, h):
            own = products.tile([P, GROUP_TOKENS], F32)
            nc.vector.scalar_tensor_tensor(
                out=own[:],
                in0=proj_tiles[(g, h)][:],
                scalar=bias[:, h : h + 1],
                in1=cos_t[:, table_columns(g)],
                op0=ALU.add,
                op1=ALU.mult,
            )
            own_tiles[(g, h)] = own

        def lent_product(g, h):
            lent = products.tile([P, GROUP_TOKENS], F32)
            nc.vector.scalar_tensor_tensor(
                out=lent[:],
                in0=proj_tiles[(g, h)][:],
                scalar=bias[:, h : h + 1],
                in1=sin_lent_t[:, table_columns(g)],
                op0=ALU.add,
                op1=ALU.mult,
            )
            lent_tiles[(g, h)] = lent

        def lent_product_beside_vector(g, h):
            biased = products.tile([P, GROUP_TOKENS], F32)
            nc.scalar.activation(out=biased[:], in_=proj_tiles[(g, h)][:], func=ACT.Identity, bias=bias[:, h : h + 1], scale=1.0)
            lent = products.tile([P, GROUP_TOKENS], F32)
            nc.gpsimd.tensor_tensor(out=lent[:], in0=biased[:], in1=sin_lent_t[:, table_columns(g)], op=ALU.mult)
            lent_tiles[(g, h)] = lent

        def finish(g, h):
            own = own_tiles[(g, h)]
            lent = lent_tiles[(g, h)]
            rope_ps = psum_rope.tile([P, GROUP_ROWS, D], F32, tag="rope")
            for j in range(GROUP_ROWS):
                block = slice(j * P, (j + 1) * P)
                nc.tensor.matmul(rope_ps[:, j, :], lhsT=own[:, block], rhs=ident_f32[:], is_transpose=True, start=True, stop=False)
                nc.tensor.matmul(rope_ps[:, j, :], lhsT=lent[:, block], rhs=swap_f32[:], is_transpose=True, start=False, stop=True)
            out_sb = results.tile([P, GROUP_ROWS, D], F32)
            nc.scalar.activation(out=out_sb[:], in_=rope_ps[:], func=ACT.Relu)
            rows = slice((g % 2) * GROUP_ROWS, (g % 2 + 1) * GROUP_ROWS)
            nc.sync.dma_start(out=out[g // 2, h].rearrange("(p j) d -> p j d", j=ROWS)[:, rows, :], in_=out_sb[:])

        def table_to_channels(table_sb, table_t):
            table_ps = psum_proj.tile([P, ROWS, P], BF16, tag="proj")
            for j in range(ROWS):
                nc.tensor.transpose(table_ps[:, j, :], table_sb[:, j, :], ident_bf16[:])
            nc.scalar.copy(out=table_t[:], in_=table_ps[:].rearrange("d j p -> d (j p)"))

        turn_tokens(0)
        cos_t = const.tile([P, S], BF16)
        table_to_channels(cos_sb, cos_t)
        turn_tokens(1)
        quantise(0)
        project(0)
        sin_lent = const.tile([P, ROWS, D], BF16)
        sin_pairs = sin_sb[:].rearrange("p j (i two) -> p j i two", two=2)
        lent_pairs = sin_lent[:].rearrange("p j (i two) -> p j i two", two=2)
        nc.gpsimd.tensor_scalar(out=lent_pairs[:, :, :, 0], in0=sin_pairs[:, :, :, 1], scalar1=1.0, scalar2=0.0, op0=ALU.mult, op1=ALU.add)
        nc.gpsimd.tensor_scalar(out=lent_pairs[:, :, :, 1], in0=sin_pairs[:, :, :, 0], scalar1=-1.0, scalar2=0.0, op0=ALU.mult, op1=ALU.add)
        sin_lent_t = const.tile([P, S], BF16)
        table_to_channels(sin_lent, sin_lent_t)
        turn_tokens(2)
        quantise(1)
        project(1)

        for g in range(GROUPS):
            lent_product_beside_vector(g, 1)
            own_product(g, 0)
            lent_product(g, 0)
            if g >= 1:
                finish(g - 1, 1)
            if g + 3 < GROUPS:
                turn_tokens(g + 3)
            if g + 2 < GROUPS:
                quantise(g + 2)
            finish(g, 0)
            if g + 2 < GROUPS:
                project(g + 2)
            own_product(g, 1)
        finish(GROUPS - 1, 1)
